import numpy as np
import ml_dtypes


def mxq(x, axis, fmt="e4m3"):
    dtype, down = {"e4m3": (ml_dtypes.float8_e4m3fn, 7), "e5m2": (ml_dtypes.float8_e5m2, 14)}[fmt]
    v = np.moveaxis(np.asarray(x, np.float32).astype(ml_dtypes.bfloat16).astype(np.float64), axis, -1)
    blocks = v.reshape(v.shape[:-1] + (-1, 32))
    amax = np.abs(blocks).max(-1, keepdims=True)
    byte = np.maximum(np.where(amax > 0, np.frexp(amax)[1] - 1 + 127, 0) - down, 1)
    scale = np.exp2(byte - 127.0)
    codes = (blocks / scale).astype(np.float32).astype(dtype).astype(np.float64)
    return np.moveaxis((codes * scale).reshape(v.shape), -1, axis)


WIDE = False


def mx_kscale(k):
    if not WIDE:
        return np.ones(k)
    levels = np.array([10, -10, 5, -5, 0])
    a = np.random.permutation(np.resize(levels, k // 512 * 4)).reshape(k // 512, 4)
    idx = np.arange(k)
    return np.exp2(a[idx // 512, idx % 128 // 32])


BF16 = ml_dtypes.bfloat16


def bf(x):
    return np.asarray(x, np.float32).astype(BF16)


def f64(x):
    return np.asarray(x).astype(np.float64)


B, S, D, BD, K = 8, 1024, 512, 512, 128
TS = 3.0


def sigmoid(v):
    return 1.0 / (1.0 + np.exp(-v))


def setup_inputs():
    s = mx_kscale(D)
    return {
        "token_embeddings": bf(np.random.standard_normal((B, S, D)) * TS * s),
        "splat_influences": bf(np.random.uniform(size=(B, S, K))),
        "decoded": bf(np.random.standard_normal((B, K, D)) * 0.35),
        "gate_W": bf(np.random.standard_normal((D, D)) / (TS * np.sqrt(D)) / s[:, None]),
        "gate_b": bf(np.random.standard_normal(D) * 0.5),
    }


def reference(token_embeddings, splat_influences, decoded, gate_W, gate_b):
    flow = f64(splat_influences) @ f64(decoded)
    gate = sigmoid((mxq(f64(token_embeddings), 2, "e4m3") @ mxq(f64(gate_W), 0, "e4m3")) + f64(gate_b))
    return flow * gate

@@ -1,0 +1,214 @@
+from contextlib import ExitStack
+
+import concourse.mybir as mybir
+from concourse.masks import make_identity
+
+F32 = mybir.dt.float32
+BF16 = mybir.dt.bfloat16
+U32 = mybir.dt.uint32
+U8 = mybir.dt.uint8
+FP8X4 = mybir.dt.float8_e4m3fn_x4
+ADD = mybir.AluOpType.add
+MULT = mybir.AluOpType.mult
+SIGMOID = mybir.ActivationFunctionType.Sigmoid
+
+P = 128
+BATCH, TOKENS, FEAT, SPLATS = 8, 1024, 512, 128
+SLOTS = TOKENS // P
+GROUP = 4
+N_TILES = BATCH * SLOTS
+N_GROUPS = N_TILES // GROUP
+FLOPS = 2 * BATCH * TOKENS * FEAT * FEAT + 2 * BATCH * TOKENS * SPLATS * FEAT
+
+POOL_EVERY = 0
+POOL_AT = 1
+
+
+def tile_splatinformationflow_pb_t_kernel(
+    tc, token_embeddings, splat_influences, decoded, gate_W, gate_b, out
+):
+    nc = tc.nc
+    x_dram = token_embeddings.rearrange("b (p j) k -> b p (j k)", j=SLOTS)
+    i_dram = splat_influences.rearrange("b (p j) s -> p b (j s)", j=SLOTS)
+    d_dram = decoded.rearrange("b s d -> s b d")
+    o_dram = out.rearrange("b (p j) d -> b p (j d)", j=SLOTS)
+
+    with ExitStack() as ctx:
+        ctx.enter_context(tc.manual_schedule())
+        const = ctx.enter_context(tc.tile_pool(name="const", bufs=1))
+        stage = ctx.enter_context(tc.tile_pool(name="stage", bufs=2))
+        zpool = ctx.enter_context(tc.tile_pool(name="zpool", bufs=3))
+        opool = ctx.enter_context(tc.tile_pool(name="opool", bufs=6))
+        ps_xt = ctx.enter_context(tc.psum_pool(name="ps_xt", bufs=2))
+        ps_it = ctx.enter_context(tc.psum_pool(name="ps_it", bufs=1))
+        ps_g = ctx.enter_context(tc.psum_pool(name="ps_g", bufs=2))
+        ps_f = ctx.enter_context(tc.psum_pool(name="ps_f", bufs=3))
+
+        x_sb = [const.tile([P, SLOTS * FEAT], BF16, name="x%d" % b) for b in range(BATCH)]
+        i_a = const.tile([P, 1, SLOTS * SPLATS], BF16)
+        i_b = const.tile([P, 3, SLOTS * SPLATS], BF16)
+        i_c = const.tile([P, 4, SLOTS * SPLATS], BF16)
+        d_a = const.tile([P, 1, FEAT], BF16)
+        d_b = const.tile([P, 7, FEAT], BF16)
+        w_raw = const.tile([P, 4, FEAT], BF16)
+        w_grp = const.tile([P, FEAT, 4], BF16, align_bytes=64)
+        w_codes = const.tile([P, FEAT], U32, align_bytes=64)
+        w_scales = const.tile([P, FEAT], U8, align_bytes=64)
+        b_row = const.tile([P, FEAT], BF16)
+        ones = const.tile([P, P], BF16)
+        bias = const.tile([P, FEAT], F32)
+        ident_f = const.tile([P, P], F32)
+        ident_b = const.tile([P, P], BF16)
+        warm = const.tile([P, 1], F32)
+
+        def infl(b):
+            if b == 0:
+                return i_a[:, 0, :]
+            if b < 4:
+                return i_b[:, b - 1, :]
+            return i_c[:, b - 4, :]
+
+        def dec(b):
+            return d_a[:, 0, :] if b == 0 else d_b[:, b - 1, :]
+
+        nc.vector.memset(warm[:], 0.0)
+        nc.vector.memset(b_row[:], 0.0)
+        nc.vector.memset(ones[:], 1.0)
+        nc.scalar.activation(out=warm[:], in_=warm[:], func=SIGMOID)
+        make_identity(nc, ident_f[:])
+        make_identity(nc, ident_b[:])
+
+        half = SLOTS * FEAT // 2
+        nc.sync.dma_start(out=x_sb[0][:, 0:half], in_=x_dram[0][:, 0:half])
+        nc.sync.dma_start(
+            out=w_raw[:].rearrange("p (u e) n -> p u e n", u=2),
+            in_=gate_W.rearrange("(u q e) n -> q u e n", u=2, e=2),
+        )
+        nc.sync.dma_start(out=b_row[0:1, :], in_=gate_b.rearrange("(o n) -> o n", o=1))
+        nc.sync.dma_start(out=i_a[:], in_=i_dram[:, 0:1, :])
+        nc.sync.dma_start(out=d_a[:], in_=d_dram[:, 0:1, :])
+        nc.sync.dma_start(out=x_sb[0][:, half:], in_=x_dram[0][:, half:])
+        nc.sync.dma_start(out=x_sb[1][:], in_=x_dram[1])
+        nc.sync.dma_start(out=i_b[:], in_=i_dram[:, 1:4, :])
+        nc.sync.dma_start(out=d_b[:], in_=d_dram[:, 1:8, :])
+        nc.sync.dma_start(out=x_sb[2][:], in_=x_dram[2])
+        nc.sync.dma_start(out=x_sb[3][:], in_=x_dram[3])
+        nc.sync.dma_start(out=i_c[:], in_=i_dram[:, 4:8, :])
+        for b in range(4, BATCH):
+            nc.sync.dma_start(out=x_sb[b][:], in_=x_dram[b])
+
+        nc.vector.tensor_copy(out=w_grp[:], in_=w_raw[:].rearrange("p t n -> p n t"))
+        nc.vector.quantize_mx(
+            out=w_codes[:].bitcast(FP8X4), scales=w_scales[:], in_=w_grp[:].rearrange("p n t -> p (n t)")
+        )
+        b_ps = ps_f.tile([P, FEAT], F32, tag="f_ps")
+        nc.tensor.matmul(out=b_ps[:], lhsT=ones[:], rhs=b_row[:], start=True, stop=True)
+        nc.vector.tensor_copy(out=bias[:], in_=b_ps[:])
+
+        xts, its, grps, codes, planes, infl_t, gs, fs, zs, o_sb = {}, {}, {}, {}, {}, {}, {}, {}, {}, {}
+
+        def transposes(g):
+            b, h = g // 2, g % 2
+            words = x_sb[b][:].bitcast(F32)
+            for a in range(2):
+                xt = ps_xt.tile([P, 2, 2, P], F32)
+                xts[(g, a)] = xt
+                for s in range(2):
+                    for u in range(2):
+                        w0 = (GROUP * h + 2 * a + s) * (FEAT // 2) + P * u
+                        nc.tensor.transpose(xt[:, s, u, :], words[:, w0 : w0 + P], ident_f[:])
+            if h == 0:
+                it = ps_it.tile([P, SLOTS, P], BF16)
+                its[b] = it
+                for j in range(SLOTS):
+                    nc.tensor.transpose(it[:, j, :], infl(b)[:, j * SPLATS : (j + 1) * SPLATS], ident_b[:])
+
+        def copy_xt(g, a):
+            if a == 0:
+                grp = stage.tile([P, GROUP * P * 4], BF16, align_bytes=64)
+                grps[g] = grp
+            dst = grps[g][:].bitcast(F32).rearrange("p (s r u) -> p s r u", s=GROUP, u=2)
+            nc.scalar.copy(out=dst[:, 2 * a : 2 * a + 2], in_=xts[(g, a)][:].rearrange("p s u r -> p s r u"))
+
+        def copy_it(b):
+            i_t = stage.tile([P, SLOTS, P], BF16)
+            infl_t[b] = i_t
+            nc.scalar.copy(out=i_t[:], in_=its[b][:])
+
+        def quantise(g):
+            cod = stage.tile([P, GROUP * P], U32, align_bytes=64)
+            pla = stage.tile([P, GROUP * P], U8, align_bytes=64)
+            codes[g], planes[g] = cod, pla
+            nc.vector.quantize_mx(out=cod[:].bitcast(FP8X4), scales=pla[:], in_=grps[g][:])
+
+        def matmuls(n):
+            g, c = n // GROUP, n % GROUP
+            cols = slice(c * P, (c + 1) * P)
+            g_ps = ps_g.tile([P, FEAT], F32)
+            gs[n] = g_ps
+            nc.tensor.matmul_mx(
+                out=g_ps[:],
+                lhsT=codes[g][:, cols].bitcast(FP8X4),
+                lhsT_scale=planes[g][:, cols],
+                rhs=w_codes[:].bitcast(FP8X4),
+                rhs_scale=w_scales[:],
+                start=True,
+                stop=True,
+            )
+            f_ps = ps_f.tile([P, FEAT], F32)
+            fs[n] = f_ps
+            b, j = n // SLOTS, n % SLOTS
+            nc.tensor.matmul(out=f_ps[:], lhsT=infl_t[b][:, j, :], rhs=dec(b), start=True, stop=True)
+
+        def add_bias(n):
+            z = zpool.tile([P, FEAT], F32)
+            zs[n] = z
+            nc.vector.tensor_tensor(out=z[:], in0=gs[n][:], in1=bias[:], op=ADD)
+
+        def sigmoid(n):
+            nc.scalar.activation(out=zs[n][:], in_=zs[n][:], func=SIGMOID)
+
+        def by_pool(n):
+            return POOL_EVERY != 0 and n % GROUP == POOL_AT
+
+        def flow_copy(n):
+            f_sb = zpool.tile([P, FEAT], F32)
+            fs[n] = (fs[n], f_sb)
+            nc.scalar.copy(out=f_sb[:], in_=fs[n][0][:])
+
+        def product(n):
+            g, c = n // GROUP, n % GROUP
+            if c == 0:
+                o = opool.tile([P, GROUP, FEAT], F32)
+                o_sb[g] = o
+            if by_pool(n):
+                nc.gpsimd.tensor_tensor(out=o_sb[g][:, c, :], in0=fs[n][1][:], in1=zs[n][:], op=MULT)
+            else:
+                nc.vector.tensor_tensor(out=o_sb[g][:, c, :], in0=fs[n][:], in1=zs[n][:], op=MULT)
+            if c == GROUP - 1:
+                b, h = g // 2, g % 2
+                width = GROUP * FEAT
+                nc.sync.dma_start(
+                    out=o_dram[b][:, h * width : (h + 1) * width], in_=o_sb[g][:].rearrange("p c d -> p (c d)")
+                )
+
+        for n in range(-7, N_TILES):
+            if 0 <= n + 2 < N_TILES:
+                matmuls(n + 2)
+            if (n + 7) % GROUP == 0 and (n + 7) // GROUP < N_GROUPS:
+                transposes((n + 7) // GROUP)
+            if (n + 6) % GROUP == 0 and (n + 6) // GROUP < N_GROUPS:
+                copy_xt((n + 6) // GROUP, 0)
+            if (n + 5) % GROUP == 0 and (n + 5) // GROUP < N_GROUPS:
+                copy_xt((n + 5) // GROUP, 1)
+            if (n + 4) % (2 * GROUP) == 0 and (n + 4) // GROUP < N_GROUPS:
+                copy_it((n + 4) // (2 * GROUP))
+            if n >= 0 and by_pool(n):
+                flow_copy(n)
+            if 0 <= n + 1 < N_TILES:
+                add_bias(n + 1)
+                sigmoid(n + 1)
+            if n >= 0:
+                product(n)
+            if (n + 4) % GROUP == 0 and (n + 4) // GROUP < N_GROUPS:
+                quantise((n + 4) // GROUP)

@@ -20,7 +20,7 @@ N_TILES = BATCH * SLOTS
 N_GROUPS = N_TILES // GROUP
 FLOPS = 2 * BATCH * TOKENS * FEAT * FEAT + 2 * BATCH * TOKENS * SPLATS * FEAT
 
-POOL_EVERY = 0
+POOL_EVERY = 1
 POOL_AT = 1
 
 

@@ -15,13 +15,13 @@ SIGMOID = mybir.ActivationFunctionType.Sigmoid
 P = 128
 BATCH, TOKENS, FEAT, SPLATS = 8, 1024, 512, 128
 SLOTS = TOKENS // P
-GROUP = 4
 N_TILES = BATCH * SLOTS
-N_GROUPS = N_TILES // GROUP
+N_PAIRS = N_TILES // 2
+STORE = 4
 FLOPS = 2 * BATCH * TOKENS * FEAT * FEAT + 2 * BATCH * TOKENS * SPLATS * FEAT
 
-POOL_EVERY = 1
-POOL_AT = 1
+POOL_TILES = (1, 4, 5, 9, 13)
+CHUNKS = 2
 
 
 def tile_splatinformationflow_pb_t_kernel(
@@ -36,12 +36,12 @@ def tile_splatinformationflow_pb_t_kernel(
     with ExitStack() as ctx:
         ctx.enter_context(tc.manual_schedule())
         const = ctx.enter_context(tc.tile_pool(name="const", bufs=1))
-        stage = ctx.enter_context(tc.tile_pool(name="stage", bufs=2))
-        zpool = ctx.enter_context(tc.tile_pool(name="zpool", bufs=3))
+        stage = ctx.enter_context(tc.tile_pool(name="stage", bufs=3))
+        zpool = ctx.enter_context(tc.tile_pool(name="zpool", bufs=6))
+        fpool = ctx.enter_context(tc.tile_pool(name="fpool", bufs=3))
         opool = ctx.enter_context(tc.tile_pool(name="opool", bufs=6))
-        ps_xt = ctx.enter_context(tc.psum_pool(name="ps_xt", bufs=2))
-        ps_it = ctx.enter_context(tc.psum_pool(name="ps_it", bufs=1))
-        ps_g = ctx.enter_context(tc.psum_pool(name="ps_g", bufs=2))
+        ps_t = ctx.enter_context(tc.psum_pool(name="ps_t", bufs=2))
+        ps_g = ctx.enter_context(tc.psum_pool(name="ps_g", bufs=3))
         ps_f = ctx.enter_context(tc.psum_pool(name="ps_f", bufs=3))
 
         x_sb = [const.tile([P, SLOTS * FEAT], BF16, name="x%d" % b) for b in range(BATCH)]
@@ -78,16 +78,17 @@ def tile_splatinformationflow_pb_t_kernel(
         make_identity(nc, ident_f[:])
         make_identity(nc, ident_b[:])
 
-        half = SLOTS * FEAT // 2
-        nc.sync.dma_start(out=x_sb[0][:, 0:half], in_=x_dram[0][:, 0:half])
+        quarter = SLOTS * FEAT // 4
+        nc.sync.dma_start(out=x_sb[0][:, 0:quarter], in_=x_dram[0][:, 0:quarter])
         nc.sync.dma_start(
             out=w_raw[:].rearrange("p (u e) n -> p u e n", u=2),
             in_=gate_W.rearrange("(u q e) n -> q u e n", u=2, e=2),
         )
         nc.sync.dma_start(out=b_row[0:1, :], in_=gate_b.rearrange("(o n) -> o n", o=1))
+        nc.sync.dma_start(out=x_sb[0][:, quarter : 2 * quarter], in_=x_dram[0][:, quarter : 2 * quarter])
         nc.sync.dma_start(out=i_a[:], in_=i_dram[:, 0:1, :])
         nc.sync.dma_start(out=d_a[:], in_=d_dram[:, 0:1, :])
-        nc.sync.dma_start(out=x_sb[0][:, half:], in_=x_dram[0][:, half:])
+        nc.sync.dma_start(out=x_sb[0][:, 2 * quarter :], in_=x_dram[0][:, 2 * quarter :])
         nc.sync.dma_start(out=x_sb[1][:], in_=x_dram[1])
         nc.sync.dma_start(out=i_b[:], in_=i_dram[:, 1:4, :])
         nc.sync.dma_start(out=d_b[:], in_=d_dram[:, 1:8, :])
@@ -97,68 +98,79 @@ def tile_splatinformationflow_pb_t_kernel(
         for b in range(4, BATCH):
             nc.sync.dma_start(out=x_sb[b][:], in_=x_dram[b])
 
-        nc.vector.tensor_copy(out=w_grp[:], in_=w_raw[:].rearrange("p t n -> p n t"))
-        nc.vector.quantize_mx(
-            out=w_codes[:].bitcast(FP8X4), scales=w_scales[:], in_=w_grp[:].rearrange("p n t -> p (n t)")
-        )
-        b_ps = ps_f.tile([P, FEAT], F32, tag="f_ps")
-        nc.tensor.matmul(out=b_ps[:], lhsT=ones[:], rhs=b_row[:], start=True, stop=True)
-        nc.vector.tensor_copy(out=bias[:], in_=b_ps[:])
+        xts, its, grps, codes, planes, infl_t, gs, fs, f_sbs, zs, o_sbs = {}, {}, {}, {}, {}, {}, {}, {}, {}, {}, {}
 
-        xts, its, grps, codes, planes, infl_t, gs, fs, zs, o_sb = {}, {}, {}, {}, {}, {}, {}, {}, {}, {}
+        def weights():
+            nc.vector.tensor_copy(out=w_grp[:], in_=w_raw[:].rearrange("p t n -> p n t"))
+            nc.vector.quantize_mx(
+                out=w_codes[:].bitcast(FP8X4), scales=w_scales[:], in_=w_grp[:].rearrange("p n t -> p (n t)")
+            )
 
-        def transposes(g):
-            b, h = g // 2, g % 2
-            words = x_sb[b][:].bitcast(F32)
-            for a in range(2):
-                xt = ps_xt.tile([P, 2, 2, P], F32)
-                xts[(g, a)] = xt
-                for s in range(2):
-                    for u in range(2):
-                        w0 = (GROUP * h + 2 * a + s) * (FEAT // 2) + P * u
-                        nc.tensor.transpose(xt[:, s, u, :], words[:, w0 : w0 + P], ident_f[:])
-            if h == 0:
-                it = ps_it.tile([P, SLOTS, P], BF16)
-                its[b] = it
-                for j in range(SLOTS):
-                    nc.tensor.transpose(it[:, j, :], infl(b)[:, j * SPLATS : (j + 1) * SPLATS], ident_b[:])
+        def bias_rows():
+            b_ps = ps_f.tile([P, FEAT], F32, tag="f_ps")
+            fs["bias"] = b_ps
+            nc.tensor.matmul(out=b_ps[:], lhsT=ones[:], rhs=b_row[:], start=True, stop=True)
 
-        def copy_xt(g, a):
-            if a == 0:
-                grp = stage.tile([P, GROUP * P * 4], BF16, align_bytes=64)
-                grps[g] = grp
-            dst = grps[g][:].bitcast(F32).rearrange("p (s r u) -> p s r u", s=GROUP, u=2)
-            nc.scalar.copy(out=dst[:, 2 * a : 2 * a + 2], in_=xts[(g, a)][:].rearrange("p s u r -> p s r u"))
+        def t_x(q):
+            words = x_sb[q // 4][:].bitcast(F32)
+            xt = ps_t.tile([P, 2, 2, P], F32, tag="t")
+            xts[q] = xt
+            for s in range(2):
+                for u in range(2):
+                    w0 = (2 * (q % 4) + s) * (FEAT // 2) + P * u
+                    nc.tensor.transpose(xt[:, s, u, :], words[:, w0 : w0 + P], ident_f[:])
 
-        def copy_it(b):
-            i_t = stage.tile([P, SLOTS, P], BF16)
+        def t_i(b):
+            it = ps_t.tile([P, SLOTS, P], BF16, tag="t")
+            its[b] = it
+            for j in range(SLOTS):
+                nc.tensor.transpose(it[:, j, :], infl(b)[:, j * SPLATS : (j + 1) * SPLATS], ident_b[:])
+
+        def c_x(q):
+            if q % 2 == 0:
+                grp = stage.tile([P, 4 * P * 4], BF16, align_bytes=64)
+                grps[q // 2] = grp
+            dst = grps[q // 2][:].bitcast(F32).rearrange("p (s r u) -> p s r u", s=4, u=2)
+            a = 2 * (q % 2)
+            nc.scalar.copy(out=dst[:, a : a + 2], in_=xts[q][:].rearrange("p s u r -> p s r u"))
+
+        def c_i(b):
+            i_t = stage.tile([P, SLOTS, P], BF16, bufs=2)
             infl_t[b] = i_t
             nc.scalar.copy(out=i_t[:], in_=its[b][:])
 
-        def quantise(g):
-            cod = stage.tile([P, GROUP * P], U32, align_bytes=64)
-            pla = stage.tile([P, GROUP * P], U8, align_bytes=64)
-            codes[g], planes[g] = cod, pla
-            nc.vector.quantize_mx(out=cod[:].bitcast(FP8X4), scales=pla[:], in_=grps[g][:])
+        def quantise(g, first, count):
+            if first == 0:
+                cod = stage.tile([P, 4 * P], U32, align_bytes=64)
+                pla = stage.tile([P, 4 * P], U8, align_bytes=64)
+                codes[g], planes[g] = cod, pla
+            cols = slice(first * P, (first + count) * P)
+            nc.vector.quantize_mx(
+                out=codes[g][:, cols].bitcast(FP8X4),
+                scales=planes[g][:, cols],
+                in_=grps[g][:, 4 * first * P : 4 * (first + count) * P],
+            )
 
-        def matmuls(n):
-            g, c = n // GROUP, n % GROUP
-            cols = slice(c * P, (c + 1) * P)
+        def mx(n):
+            cols = slice((n % 4) * P, (n % 4 + 1) * P)
             g_ps = ps_g.tile([P, FEAT], F32)
             gs[n] = g_ps
             nc.tensor.matmul_mx(
                 out=g_ps[:],
-                lhsT=codes[g][:, cols].bitcast(FP8X4),
-                lhsT_scale=planes[g][:, cols],
+                lhsT=codes[n // 4][:, cols].bitcast(FP8X4),
+                lhsT_scale=planes[n // 4][:, cols],
                 rhs=w_codes[:].bitcast(FP8X4),
                 rhs_scale=w_scales[:],
                 start=True,
                 stop=True,
             )
+
+        def plain(n):
             f_ps = ps_f.tile([P, FEAT], F32)
             fs[n] = f_ps
-            b, j = n // SLOTS, n % SLOTS
-            nc.tensor.matmul(out=f_ps[:], lhsT=infl_t[b][:, j, :], rhs=dec(b), start=True, stop=True)
+            nc.tensor.matmul(
+                out=f_ps[:], lhsT=infl_t[n // SLOTS][:, n % SLOTS, :], rhs=dec(n // SLOTS), start=True, stop=True
+            )
 
         def add_bias(n):
             z = zpool.tile([P, FEAT], F32)
@@ -169,46 +181,73 @@ def tile_splatinformationflow_pb_t_kernel(
             nc.scalar.activation(out=zs[n][:], in_=zs[n][:], func=SIGMOID)
 
         def by_pool(n):
-            return POOL_EVERY != 0 and n % GROUP == POOL_AT
+            return n % 16 in POOL_TILES
 
         def flow_copy(n):
-            f_sb = zpool.tile([P, FEAT], F32)
-            fs[n] = (fs[n], f_sb)
-            nc.scalar.copy(out=f_sb[:], in_=fs[n][0][:])
+            f_sb = fpool.tile([P, FEAT], F32)
+            f_sbs[n] = f_sb
+            nc.scalar.copy(out=f_sb[:], in_=fs[n][:])
 
         def product(n):
-            g, c = n // GROUP, n % GROUP
+            g, c = n // STORE, n % STORE
             if c == 0:
-                o = opool.tile([P, GROUP, FEAT], F32)
-                o_sb[g] = o
+                o = opool.tile([P, STORE, FEAT], F32)
+                o_sbs[g] = o
             if by_pool(n):
-                nc.gpsimd.tensor_tensor(out=o_sb[g][:, c, :], in0=fs[n][1][:], in1=zs[n][:], op=MULT)
+                w = FEAT // CHUNKS
+                for i in range(CHUNKS):
+                    cs = slice(i * w, (i + 1) * w)
+                    nc.gpsimd.tensor_tensor(out=o_sbs[g][:, c, cs], in0=f_sbs[n][:, cs], in1=zs[n][:, cs], op=MULT)
             else:
-                nc.vector.tensor_tensor(out=o_sb[g][:, c, :], in0=fs[n][:], in1=zs[n][:], op=MULT)
-            if c == GROUP - 1:
-                b, h = g // 2, g % 2
-                width = GROUP * FEAT
-                nc.sync.dma_start(
-                    out=o_dram[b][:, h * width : (h + 1) * width], in_=o_sb[g][:].rearrange("p c d -> p (c d)")
-                )
+                nc.vector.tensor_tensor(out=o_sbs[g][:, c, :], in0=fs[n][:], in1=zs[n][:], op=MULT)
 
-        for n in range(-7, N_TILES):
-            if 0 <= n + 2 < N_TILES:
-                matmuls(n + 2)
-            if (n + 7) % GROUP == 0 and (n + 7) // GROUP < N_GROUPS:
-                transposes((n + 7) // GROUP)
-            if (n + 6) % GROUP == 0 and (n + 6) // GROUP < N_GROUPS:
-                copy_xt((n + 6) // GROUP, 0)
-            if (n + 5) % GROUP == 0 and (n + 5) // GROUP < N_GROUPS:
-                copy_xt((n + 5) // GROUP, 1)
-            if (n + 4) % (2 * GROUP) == 0 and (n + 4) // GROUP < N_GROUPS:
-                copy_it((n + 4) // (2 * GROUP))
-            if n >= 0 and by_pool(n):
-                flow_copy(n)
-            if 0 <= n + 1 < N_TILES:
-                add_bias(n + 1)
+        def store(n0, n1):
+            b, g = n0 // SLOTS, n0 // STORE
+            nc.sync.dma_start(
+                out=o_dram[b][:, (n0 % SLOTS) * FEAT : (n0 % SLOTS + n1 - n0) * FEAT],
+                in_=o_sbs[g][:, n0 % STORE : n0 % STORE + n1 - n0, :].rearrange("p c d -> p (c d)"),
+            )
+
+        def tile_ok(n):
+            return 0 <= n < N_TILES
+
+        for n in range(-9, N_TILES + 1):
+            if tile_ok(n + 4):
+                mx(n + 4)
+            if tile_ok(n + 2):
+                plain(n + 2)
+            if (n + 9) % 2 == 0 and 0 <= (n + 9) // 2 < N_PAIRS:
+                t_x((n + 9) // 2)
+            if n == -9:
+                bias_rows()
+            if (n + 6) % 8 == 0 and 0 <= (n + 6) // 8 < BATCH:
+                t_i((n + 6) // 8)
+            if tile_ok(n + 1):
                 sigmoid(n + 1)
-            if n >= 0:
+            if (n + 8) % 2 == 0 and 0 <= (n + 8) // 2 < N_PAIRS:
+                c_x((n + 8) // 2)
+            if (n + 5) % 8 == 0 and 0 <= (n + 5) // 8 < BATCH:
+                c_i((n + 5) // 8)
+            if tile_ok(n) and by_pool(n):
+                flow_copy(n)
+            if n == -8:
+                weights()
+            if tile_ok(n + 2):
+                add_bias(n + 2)
+            if tile_ok(n):
                 product(n)
-            if (n + 4) % GROUP == 0 and (n + 4) // GROUP < N_GROUPS:
-                quantise((n + 4) // GROUP)
+            if n == -7:
+                quantise(0, 0, 2)
+            if n == -6:
+                nc.vector.tensor_copy(out=bias[:], in_=fs["bias"][:])
+            if n == -5:
+                quantise(0, 2, 2)
+            if (n + 5) % 4 == 0 and 1 <= (n + 5) // 4 < N_TILES // 4:
+                quantise((n + 5) // 4, 0, 4)
+            if tile_ok(n - 1) and (n - 1) % STORE == STORE - 1 and n - 1 < N_TILES - STORE:
+                store(n - STORE, n)
+            if n == N_TILES - 2:
+                store(n - 2, n)
+                store(n, n + 1)
+            if n == N_TILES - 1:
+                store(n, n + 1)

@@ -20,7 +20,8 @@ N_PAIRS = N_TILES // 2
 STORE = 4
 FLOPS = 2 * BATCH * TOKENS * FEAT * FEAT + 2 * BATCH * TOKENS * SPLATS * FEAT
 
-POOL_TILES = (1, 4, 5, 9, 13)
+POOL_TILES = (3, 7, 11, 15, 5, 13)
+POOL_TAIL = (56, 58)
 CHUNKS = 2
 
 
@@ -79,16 +80,16 @@ def tile_splatinformationflow_pb_t_kernel(
         make_identity(nc, ident_b[:])
 
         quarter = SLOTS * FEAT // 4
-        nc.sync.dma_start(out=x_sb[0][:, 0:quarter], in_=x_dram[0][:, 0:quarter])
         nc.sync.dma_start(
             out=w_raw[:].rearrange("p (u e) n -> p u e n", u=2),
             in_=gate_W.rearrange("(u q e) n -> q u e n", u=2, e=2),
         )
         nc.sync.dma_start(out=b_row[0:1, :], in_=gate_b.rearrange("(o n) -> o n", o=1))
+        nc.sync.dma_start(out=x_sb[0][:, 0:quarter], in_=x_dram[0][:, 0:quarter])
         nc.sync.dma_start(out=x_sb[0][:, quarter : 2 * quarter], in_=x_dram[0][:, quarter : 2 * quarter])
+        nc.sync.dma_start(out=x_sb[0][:, 2 * quarter :], in_=x_dram[0][:, 2 * quarter :])
         nc.sync.dma_start(out=i_a[:], in_=i_dram[:, 0:1, :])
         nc.sync.dma_start(out=d_a[:], in_=d_dram[:, 0:1, :])
-        nc.sync.dma_start(out=x_sb[0][:, 2 * quarter :], in_=x_dram[0][:, 2 * quarter :])
         nc.sync.dma_start(out=x_sb[1][:], in_=x_dram[1])
         nc.sync.dma_start(out=i_b[:], in_=i_dram[:, 1:4, :])
         nc.sync.dma_start(out=d_b[:], in_=d_dram[:, 1:8, :])
@@ -181,7 +182,7 @@ def tile_splatinformationflow_pb_t_kernel(
             nc.scalar.activation(out=zs[n][:], in_=zs[n][:], func=SIGMOID)
 
         def by_pool(n):
-            return n % 16 in POOL_TILES
+            return (n % 16 in POOL_TILES and n < 56) or n in POOL_TAIL
 
         def flow_copy(n):
             f_sb = fpool.tile([P, FEAT], F32)
@@ -220,22 +221,24 @@ def tile_splatinformationflow_pb_t_kernel(
                 t_x((n + 9) // 2)
             if n == -9:
                 bias_rows()
-            if (n + 6) % 8 == 0 and 0 <= (n + 6) // 8 < BATCH:
-                t_i((n + 6) // 8)
+            if n == -4:
+                t_i(0)
+            if (n + 8) % 8 == 0 and 1 <= (n + 8) // 8 < BATCH:
+                t_i((n + 8) // 8)
             if tile_ok(n + 1):
                 sigmoid(n + 1)
             if (n + 8) % 2 == 0 and 0 <= (n + 8) // 2 < N_PAIRS:
                 c_x((n + 8) // 2)
-            if (n + 5) % 8 == 0 and 0 <= (n + 5) // 8 < BATCH:
-                c_i((n + 5) // 8)
+            if n == -3:
+                c_i(0)
+            if (n + 7) % 8 == 0 and 1 <= (n + 7) // 8 < BATCH:
+                c_i((n + 7) // 8)
             if tile_ok(n) and by_pool(n):
                 flow_copy(n)
             if n == -8:
                 weights()
             if tile_ok(n + 2):
                 add_bias(n + 2)
-            if tile_ok(n):
-                product(n)
             if n == -7:
                 quantise(0, 0, 2)
             if n == -6:
@@ -244,10 +247,9 @@ def tile_splatinformationflow_pb_t_kernel(
                 quantise(0, 2, 2)
             if (n + 5) % 4 == 0 and 1 <= (n + 5) // 4 < N_TILES // 4:
                 quantise((n + 5) // 4, 0, 4)
-            if tile_ok(n - 1) and (n - 1) % STORE == STORE - 1 and n - 1 < N_TILES - STORE:
-                store(n - STORE, n)
-            if n == N_TILES - 2:
+            if tile_ok(n):
+                product(n)
+            if tile_ok(n - 1) and (n - 1) % 2 == 1 and n - 1 < N_TILES - STORE:
                 store(n - 2, n)
-                store(n, n + 1)
-            if n == N_TILES - 1:
+            if n >= N_TILES - STORE and tile_ok(n):
                 store(n, n + 1)

@@ -20,7 +20,7 @@ N_PAIRS = N_TILES // 2
 STORE = 4
 FLOPS = 2 * BATCH * TOKENS * FEAT * FEAT + 2 * BATCH * TOKENS * SPLATS * FEAT
 
-POOL_TILES = (3, 7, 11, 15, 5, 13)
+POOL_TILES = (1, 3, 5, 7, 9, 11, 15)
 POOL_TAIL = (56, 58)
 CHUNKS = 2
 
@@ -138,7 +138,7 @@ def tile_splatinformationflow_pb_t_kernel(
         def c_i(b):
             i_t = stage.tile([P, SLOTS, P], BF16, bufs=2)
             infl_t[b] = i_t
-            nc.scalar.copy(out=i_t[:], in_=its[b][:])
+            nc.vector.tensor_copy(out=i_t[:], in_=its[b][:])
 
         def quantise(g, first, count):
             if first == 0:
@@ -213,10 +213,10 @@ def tile_splatinformationflow_pb_t_kernel(
             return 0 <= n < N_TILES
 
         for n in range(-9, N_TILES + 1):
-            if tile_ok(n + 4):
-                mx(n + 4)
             if tile_ok(n + 2):
                 plain(n + 2)
+            if tile_ok(n + 4):
+                mx(n + 4)
             if (n + 9) % 2 == 0 and 0 <= (n + 9) // 2 < N_PAIRS:
                 t_x((n + 9) // 2)
             if n == -9:
@@ -229,16 +229,16 @@ def tile_splatinformationflow_pb_t_kernel(
                 sigmoid(n + 1)
             if (n + 8) % 2 == 0 and 0 <= (n + 8) // 2 < N_PAIRS:
                 c_x((n + 8) // 2)
-            if n == -3:
-                c_i(0)
-            if (n + 7) % 8 == 0 and 1 <= (n + 7) // 8 < BATCH:
-                c_i((n + 7) // 8)
             if tile_ok(n) and by_pool(n):
                 flow_copy(n)
             if n == -8:
                 weights()
             if tile_ok(n + 2):
                 add_bias(n + 2)
+            if n == -3:
+                c_i(0)
+            if (n + 6) % 8 == 0 and 1 <= (n + 6) // 8 < BATCH:
+                c_i((n + 6) // 8)
             if n == -7:
                 quantise(0, 0, 2)
             if n == -6:

@@ -20,9 +20,11 @@ N_PAIRS = N_TILES // 2
 STORE = 4
 FLOPS = 2 * BATCH * TOKENS * FEAT * FEAT + 2 * BATCH * TOKENS * SPLATS * FEAT
 
-POOL_TILES = (1, 3, 5, 7, 9, 11, 15)
+POOL_TILES = (0, 1, 4, 8, 9, 12)
 POOL_TAIL = (56, 58)
 CHUNKS = 2
+FENCE = True
+POOL_FROM = 4
 
 
 def tile_splatinformationflow_pb_t_kernel(
@@ -138,7 +140,7 @@ def tile_splatinformationflow_pb_t_kernel(
         def c_i(b):
             i_t = stage.tile([P, SLOTS, P], BF16, bufs=2)
             infl_t[b] = i_t
-            nc.vector.tensor_copy(out=i_t[:], in_=its[b][:])
+            nc.scalar.copy(out=i_t[:], in_=its[b][:])
 
         def quantise(g, first, count):
             if first == 0:
@@ -182,7 +184,7 @@ def tile_splatinformationflow_pb_t_kernel(
             nc.scalar.activation(out=zs[n][:], in_=zs[n][:], func=SIGMOID)
 
         def by_pool(n):
-            return (n % 16 in POOL_TILES and n < 56) or n in POOL_TAIL
+            return (n % 16 in POOL_TILES and POOL_FROM <= n < 56) or n in POOL_TAIL
 
         def flow_copy(n):
             f_sb = fpool.tile([P, FEAT], F32)
@@ -212,43 +214,45 @@ def tile_splatinformationflow_pb_t_kernel(
         def tile_ok(n):
             return 0 <= n < N_TILES
 
-        for n in range(-9, N_TILES + 1):
+        for n in range(-10, N_TILES + 1):
             if tile_ok(n + 2):
                 plain(n + 2)
             if tile_ok(n + 4):
                 mx(n + 4)
-            if (n + 9) % 2 == 0 and 0 <= (n + 9) // 2 < N_PAIRS:
-                t_x((n + 9) // 2)
-            if n == -9:
+            if (n + 10) % 2 == 0 and 0 <= (n + 10) // 2 < N_PAIRS:
+                t_x((n + 10) // 2)
+            if n == -10:
                 bias_rows()
             if n == -4:
                 t_i(0)
-            if (n + 8) % 8 == 0 and 1 <= (n + 8) // 8 < BATCH:
-                t_i((n + 8) // 8)
+            if (n + 7) % 8 == 0 and 1 <= (n + 7) // 8 < BATCH:
+                t_i((n + 7) // 8)
             if tile_ok(n + 1):
                 sigmoid(n + 1)
-            if (n + 8) % 2 == 0 and 0 <= (n + 8) // 2 < N_PAIRS:
-                c_x((n + 8) // 2)
-            if tile_ok(n) and by_pool(n):
-                flow_copy(n)
-            if n == -8:
-                weights()
-            if tile_ok(n + 2):
-                add_bias(n + 2)
+            if (n + 9) % 2 == 0 and 0 <= (n + 9) // 2 < N_PAIRS:
+                c_x((n + 9) // 2)
             if n == -3:
                 c_i(0)
             if (n + 6) % 8 == 0 and 1 <= (n + 6) // 8 < BATCH:
                 c_i((n + 6) // 8)
+            if tile_ok(n + 1) and by_pool(n + 1):
+                flow_copy(n + 1)
+            if n == -9:
+                weights()
+            if tile_ok(n + 2):
+                add_bias(n + 2)
             if n == -7:
                 quantise(0, 0, 2)
             if n == -6:
                 nc.vector.tensor_copy(out=bias[:], in_=fs["bias"][:])
             if n == -5:
                 quantise(0, 2, 2)
-            if (n + 5) % 4 == 0 and 1 <= (n + 5) // 4 < N_TILES // 4:
-                quantise((n + 5) // 4, 0, 4)
             if tile_ok(n):
                 product(n)
+            if (n + 5) % 4 == 0 and 1 <= (n + 5) // 4 < N_TILES // 4:
+                quantise((n + 5) // 4, 0, 4)
+                if FENCE:
+                    nc.gpsimd.memset(grps[(n + 5) // 4][:, 0:2], 0.0)
             if tile_ok(n - 1) and (n - 1) % 2 == 1 and n - 1 < N_TILES - STORE:
                 store(n - 2, n)
             if n >= N_TILES - STORE and tile_ok(n):

from contextlib import ExitStack

import concourse.mybir as mybir
from concourse.masks import make_identity

F32 = mybir.dt.float32
BF16 = mybir.dt.bfloat16
U32 = mybir.dt.uint32
U8 = mybir.dt.uint8
FP8X4 = mybir.dt.float8_e4m3fn_x4
ADD = mybir.AluOpType.add
MULT = mybir.AluOpType.mult
SIGMOID = mybir.ActivationFunctionType.Sigmoid

P = 128
BATCH, TOKENS, FEAT, SPLATS = 8, 1024, 512, 128
SLOTS = TOKENS // P
N_TILES = BATCH * SLOTS
N_PAIRS = N_TILES // 2
STORE = 4
FLOPS = 2 * BATCH * TOKENS * FEAT * FEAT + 2 * BATCH * TOKENS * SPLATS * FEAT

POOL_TILES = (0, 1, 4, 8, 9, 12)
POOL_TAIL = (56, 58)
CHUNKS = 2
FENCE = True
POOL_FROM = 4


def tile_splatinformationflow_pb_t_kernel(
    tc, token_embeddings, splat_influences, decoded, gate_W, gate_b, out
):
    nc = tc.nc
    x_dram = token_embeddings.rearrange("b (p j) k -> b p (j k)", j=SLOTS)
    i_dram = splat_influences.rearrange("b (p j) s -> p b (j s)", j=SLOTS)
    d_dram = decoded.rearrange("b s d -> s b d")
    o_dram = out.rearrange("b (p j) d -> b p (j d)", j=SLOTS)

    with ExitStack() as ctx:
        ctx.enter_context(tc.manual_schedule())
        const = ctx.enter_context(tc.tile_pool(name="const", bufs=1))
        stage = ctx.enter_context(tc.tile_pool(name="stage", bufs=3))
        zpool = ctx.enter_context(tc.tile_pool(name="zpool", bufs=6))
        fpool = ctx.enter_context(tc.tile_pool(name="fpool", bufs=3))
        opool = ctx.enter_context(tc.tile_pool(name="opool", bufs=6))
        ps_t = ctx.enter_context(tc.psum_pool(name="ps_t", bufs=2))
        ps_g = ctx.enter_context(tc.psum_pool(name="ps_g", bufs=3))
        ps_f = ctx.enter_context(tc.psum_pool(name="ps_f", bufs=3))

        x_sb = [const.tile([P, SLOTS * FEAT], BF16, name="x%d" % b) for b in range(BATCH)]
        i_a = const.tile([P, 1, SLOTS * SPLATS], BF16)
        i_b = const.tile([P, 3, SLOTS * SPLATS], BF16)
        i_c = const.tile([P, 4, SLOTS * SPLATS], BF16)
        d_a = const.tile([P, 1, FEAT], BF16)
        d_b = const.tile([P, 7, FEAT], BF16)
        w_raw = const.tile([P, 4, FEAT], BF16)
        w_grp = const.tile([P, FEAT, 4], BF16, align_bytes=64)
        w_codes = const.tile([P, FEAT], U32, align_bytes=64)
        w_scales = const.tile([P, FEAT], U8, align_bytes=64)
        b_row = const.tile([P, FEAT], BF16)
        ones = const.tile([P, P], BF16)
        bias = const.tile([P, FEAT], F32)
        ident_f = const.tile([P, P], F32)
        ident_b = const.tile([P, P], BF16)
        warm = const.tile([P, 1], F32)

        def infl(b):
            if b == 0:
                return i_a[:, 0, :]
            if b < 4:
                return i_b[:, b - 1, :]
            return i_c[:, b - 4, :]

        def dec(b):
            return d_a[:, 0, :] if b == 0 else d_b[:, b - 1, :]

        nc.vector.memset(warm[:], 0.0)
        nc.vector.memset(b_row[:], 0.0)
        nc.vector.memset(ones[:], 1.0)
        nc.scalar.activation(out=warm[:], in_=warm[:], func=SIGMOID)
        make_identity(nc, ident_f[:])
        make_identity(nc, ident_b[:])

        quarter = SLOTS * FEAT // 4
        nc.sync.dma_start(
            out=w_raw[:].rearrange("p (u e) n -> p u e n", u=2),
            in_=gate_W.rearrange("(u q e) n -> q u e n", u=2, e=2),
        )
        nc.sync.dma_start(out=b_row[0:1, :], in_=gate_b.rearrange("(o n) -> o n", o=1))
        nc.sync.dma_start(out=x_sb[0][:, 0:quarter], in_=x_dram[0][:, 0:quarter])
        nc.sync.dma_start(out=x_sb[0][:, quarter : 2 * quarter], in_=x_dram[0][:, quarter : 2 * quarter])
        nc.sync.dma_start(out=x_sb[0][:, 2 * quarter :], in_=x_dram[0][:, 2 * quarter :])
        nc.sync.dma_start(out=i_a[:], in_=i_dram[:, 0:1, :])
        nc.sync.dma_start(out=d_a[:], in_=d_dram[:, 0:1, :])
        nc.sync.dma_start(out=x_sb[1][:], in_=x_dram[1])
        nc.sync.dma_start(out=i_b[:], in_=i_dram[:, 1:4, :])
        nc.sync.dma_start(out=d_b[:], in_=d_dram[:, 1:8, :])
        nc.sync.dma_start(out=x_sb[2][:], in_=x_dram[2])
        nc.sync.dma_start(out=x_sb[3][:], in_=x_dram[3])
        nc.sync.dma_start(out=i_c[:], in_=i_dram[:, 4:8, :])
        for b in range(4, BATCH):
            nc.sync.dma_start(out=x_sb[b][:], in_=x_dram[b])

        xts, its, grps, codes, planes, infl_t, gs, fs, f_sbs, zs, o_sbs = {}, {}, {}, {}, {}, {}, {}, {}, {}, {}, {}

        def weights():
            nc.vector.tensor_copy(out=w_grp[:], in_=w_raw[:].rearrange("p t n -> p n t"))
            nc.vector.quantize_mx(
                out=w_codes[:].bitcast(FP8X4), scales=w_scales[:], in_=w_grp[:].rearrange("p n t -> p (n t)")
            )

        def bias_rows():
            b_ps = ps_f.tile([P, FEAT], F32, tag="f_ps")
            fs["bias"] = b_ps
            nc.tensor.matmul(out=b_ps[:], lhsT=ones[:], rhs=b_row[:], start=True, stop=True)

        def t_x(q):
            words = x_sb[q // 4][:].bitcast(F32)
            xt = ps_t.tile([P, 2, 2, P], F32, tag="t")
            xts[q] = xt
            for s in range(2):
                for u in range(2):
                    w0 = (2 * (q % 4) + s) * (FEAT // 2) + P * u
                    nc.tensor.transpose(xt[:, s, u, :], words[:, w0 : w0 + P], ident_f[:])

        def t_i(b):
            it = ps_t.tile([P, SLOTS, P], BF16, tag="t")
            its[b] = it
            for j in range(SLOTS):
                nc.tensor.transpose(it[:, j, :], infl(b)[:, j * SPLATS : (j + 1) * SPLATS], ident_b[:])

        def c_x(q):
            if q % 2 == 0:
                grp = stage.tile([P, 4 * P * 4], BF16, align_bytes=64)
                grps[q // 2] = grp
            dst = grps[q // 2][:].bitcast(F32).rearrange("p (s r u) -> p s r u", s=4, u=2)
            a = 2 * (q % 2)
            nc.scalar.copy(out=dst[:, a : a + 2], in_=xts[q][:].rearrange("p s u r -> p s r u"))

        def c_i(b):
            i_t = stage.tile([P, SLOTS, P], BF16, bufs=2)
            infl_t[b] = i_t
            nc.scalar.copy(out=i_t[:], in_=its[b][:])

        def quantise(g, first, count):
            if first == 0:
                cod = stage.tile([P, 4 * P], U32, align_bytes=64)
                pla = stage.tile([P, 4 * P], U8, align_bytes=64)
                codes[g], planes[g] = cod, pla
            cols = slice(first * P, (first + count) * P)
            nc.vector.quantize_mx(
                out=codes[g][:, cols].bitcast(FP8X4),
                scales=planes[g][:, cols],
                in_=grps[g][:, 4 * first * P : 4 * (first + count) * P],
            )

        def mx(n):
            cols = slice((n % 4) * P, (n % 4 + 1) * P)
            g_ps = ps_g.tile([P, FEAT], F32)
            gs[n] = g_ps
            nc.tensor.matmul_mx(
                out=g_ps[:],
                lhsT=codes[n // 4][:, cols].bitcast(FP8X4),
                lhsT_scale=planes[n // 4][:, cols],
                rhs=w_codes[:].bitcast(FP8X4),
                rhs_scale=w_scales[:],
                start=True,
                stop=True,
            )

        def plain(n):
            f_ps = ps_f.tile([P, FEAT], F32)
            fs[n] = f_ps
            nc.tensor.matmul(
                out=f_ps[:], lhsT=infl_t[n // SLOTS][:, n % SLOTS, :], rhs=dec(n // SLOTS), start=True, stop=True
            )

        def add_bias(n):
            z = zpool.tile([P, FEAT], F32)
            zs[n] = z
            nc.vector.tensor_tensor(out=z[:], in0=gs[n][:], in1=bias[:], op=ADD)

        def sigmoid(n):
            nc.scalar.activation(out=zs[n][:], in_=zs[n][:], func=SIGMOID)

        def by_pool(n):
            return (n % 16 in POOL_TILES and POOL_FROM <= n < 56) or n in POOL_TAIL

        def flow_copy(n):
            f_sb = fpool.tile([P, FEAT], F32)
            f_sbs[n] = f_sb
            nc.scalar.copy(out=f_sb[:], in_=fs[n][:])

        def product(n):
            g, c = n // STORE, n % STORE
            if c == 0:
                o = opool.tile([P, STORE, FEAT], F32)
                o_sbs[g] = o
            if by_pool(n):
                w = FEAT // CHUNKS
                for i in range(CHUNKS):
                    cs = slice(i * w, (i + 1) * w)
                    nc.gpsimd.tensor_tensor(out=o_sbs[g][:, c, cs], in0=f_sbs[n][:, cs], in1=zs[n][:, cs], op=MULT)
            else:
                nc.vector.tensor_tensor(out=o_sbs[g][:, c, :], in0=fs[n][:], in1=zs[n][:], op=MULT)

        def store(n0, n1):
            b, g = n0 // SLOTS, n0 // STORE
            nc.sync.dma_start(
                out=o_dram[b][:, (n0 % SLOTS) * FEAT : (n0 % SLOTS + n1 - n0) * FEAT],
                in_=o_sbs[g][:, n0 % STORE : n0 % STORE + n1 - n0, :].rearrange("p c d -> p (c d)"),
            )

        def tile_ok(n):
            return 0 <= n < N_TILES

        for n in range(-10, N_TILES + 1):
            if tile_ok(n + 2):
                plain(n + 2)
            if tile_ok(n + 4):
                mx(n + 4)
            if (n + 10) % 2 == 0 and 0 <= (n + 10) // 2 < N_PAIRS:
                t_x((n + 10) // 2)
            if n == -10:
                bias_rows()
            if n == -4:
                t_i(0)
            if (n + 7) % 8 == 0 and 1 <= (n + 7) // 8 < BATCH:
                t_i((n + 7) // 8)
            if tile_ok(n + 1):
                sigmoid(n + 1)
            if (n + 9) % 2 == 0 and 0 <= (n + 9) // 2 < N_PAIRS:
                c_x((n + 9) // 2)
            if n == -3:
                c_i(0)
            if (n + 6) % 8 == 0 and 1 <= (n + 6) // 8 < BATCH:
                c_i((n + 6) // 8)
            if tile_ok(n + 1) and by_pool(n + 1):
                flow_copy(n + 1)
            if n == -9:
                weights()
            if tile_ok(n + 2):
                add_bias(n + 2)
            if n == -7:
                quantise(0, 0, 2)
            if n == -6:
                nc.vector.tensor_copy(out=bias[:], in_=fs["bias"][:])
            if n == -5:
                quantise(0, 2, 2)
            if tile_ok(n):
                product(n)
            if (n + 5) % 4 == 0 and 1 <= (n + 5) // 4 < N_TILES // 4:
                quantise((n + 5) // 4, 0, 4)
                if FENCE:
                    nc.gpsimd.memset(grps[(n + 5) // 4][:, 0:2], 0.0)
            if tile_ok(n - 1) and (n - 1) % 2 == 1 and n - 1 < N_TILES - STORE:
                store(n - 2, n)
            if n >= N_TILES - STORE and tile_ok(n):
                store(n, n + 1)
